import numpy as np
import ml_dtypes


def mxq(x, axis, fmt="e4m3"):
    dtype, down = {"e4m3": (ml_dtypes.float8_e4m3fn, 7), "e5m2": (ml_dtypes.float8_e5m2, 14)}[fmt]
    v = np.moveaxis(np.asarray(x, np.float32).astype(ml_dtypes.bfloat16).astype(np.float64), axis, -1)
    blocks = v.reshape(v.shape[:-1] + (-1, 32))
    amax = np.abs(blocks).max(-1, keepdims=True)
    byte = np.maximum(np.where(amax > 0, np.frexp(amax)[1] - 1 + 127, 0) - down, 1)
    scale = np.exp2(byte - 127.0)
    codes = (blocks / scale).astype(np.float32).astype(dtype).astype(np.float64)
    return np.moveaxis((codes * scale).reshape(v.shape), -1, axis)


WIDE = False


def mx_kscale(k):
    if not WIDE:
        return np.ones(k)
    levels = np.array([10, -10, 5, -5, 0])
    a = np.random.permutation(np.resize(levels, k // 512 * 4)).reshape(k // 512, 4)
    idx = np.arange(k)
    return np.exp2(a[idx // 512, idx % 128 // 32])


BF16 = ml_dtypes.bfloat16


def bf(x):
    return np.asarray(x, np.float32).astype(BF16)


def f64(x):
    return np.asarray(x).astype(np.float64)


B, C, T, O, KW = 2, 512, 512, 512, 3

EPS = 1e-8


def cosine_sim(a, b):
    na = np.maximum(np.sqrt(np.sum(a * a, axis=1)), EPS)
    nb = np.maximum(np.sqrt(np.sum(b * b, axis=1)), EPS)
    return np.sum(a * b, axis=1) / (na * nb)


def setup_inputs():
    s = mx_kscale(C)
    z = np.random.standard_normal((B, C, T + 1))
    m = np.random.standard_normal((B, 1, T))
    return {"feature": bf(np.random.standard_normal((B, C, T)) * s[None, :, None]),
            "embedding": bf(z[:, :, 1:] + m * z[:, :, :-1]),
            "weight": bf(np.random.standard_normal((O, C, KW)) / np.sqrt(C) / s[None, :, None])}


def reference(feature, embedding, weight):
    feature, embedding, weight = f64(feature), f64(embedding), f64(weight)
    emb_l = np.pad(embedding[:, :, :-1], ((0, 0), (0, 0), (1, 0)))
    emb_r = np.pad(embedding[:, :, 1:], ((0, 0), (0, 0), (0, 1)))
    sim = np.stack([cosine_sim(embedding, emb_l), cosine_sim(embedding, embedding), cosine_sim(embedding, emb_r)], axis=1)
    att = np.repeat(sim, C, axis=1)
    f_pad = np.pad(feature, ((0, 0), (0, 0), (1, 1)))
    inp_unf = np.stack([f_pad[:, :, k:k + T] for k in range(KW)], axis=2).reshape(B, C * KW, T)
    w_flat = weight.reshape(O, C * KW)
    xa = mxq(inp_unf * att, 1, "e4m3")
    return mxq(w_flat, 1, "e4m3") @ xa

@@ -1,0 +1,215 @@
+from contextlib import ExitStack
+
+import concourse.mybir as mybir
+from concourse.masks import make_identity
+
+F32 = mybir.dt.float32
+BF16 = mybir.dt.bfloat16
+U32 = mybir.dt.uint32
+U8 = mybir.dt.uint8
+FP8X4 = mybir.dt.float8_e4m3fn_x4
+ALU = mybir.AluOpType
+ACT = mybir.ActivationFunctionType
+AX = mybir.AxisListType
+
+B, C, T, O, KW = 2, 512, 512, 512, 3
+P = 128
+EPS = 1e-8
+FLOPS = 2 * B * O * T * C * KW
+
+PAD = 16
+ROW = PAD + T + PAD
+NT = T // P
+GW = 130
+G0 = 43
+
+
+def tile_attentionconv1d_kernel(tc, feature, embedding, weight, out):
+    nc = tc.nc
+    with ExitStack() as ctx:
+        const = ctx.enter_context(tc.tile_pool(name="const", bufs=1))
+        data = ctx.enter_context(tc.tile_pool(name="data", bufs=1))
+        work = ctx.enter_context(tc.tile_pool(name="work", bufs=2))
+        outp = ctx.enter_context(tc.tile_pool(name="outp", bufs=4))
+        psum = ctx.enter_context(tc.psum_pool(name="psum", bufs=1))
+
+        def bank(i, shape, name):
+            return psum.tile(shape, F32, tag="bk%d" % i, name=name)
+
+        warm = const.tile([P, 2], F32, name="warm")
+        nc.vector.memset(warm[:, 0:1], 1.0)
+        nc.scalar.activation(out=warm[:, 1:2], in_=warm[:, 0:1], func=ACT.Sqrt)
+
+        ident = const.tile([P, P], F32, name="ident")
+        make_identity(nc, ident[:])
+        mask2 = const.tile([P, 2, GW], F32, name="mask2")
+        nc.vector.memset(mask2[:], 0.0)
+        corner = const.tile([P, 2, P], F32, name="corner")
+        nc.vector.memset(corner[:], 0.0)
+
+        e_sb = [data.tile([P, 4, ROW], BF16, name="e%d" % b) for b in range(B)]
+        f_sb = [data.tile([P, 12, ROW], BF16, name="f%d" % b) for b in range(B)]
+        redpad = [data.tile([P, NT + 2, 2], F32, name="red%d" % b) for b in range(B)]
+        for b in range(B):
+            nc.vector.memset(e_sb[b][:, :, 0:PAD], 0.0)
+            nc.vector.memset(e_sb[b][:, :, PAD + T:ROW], 0.0)
+            fv = f_sb[b][:].rearrange("p (a k) q -> p a k q", k=KW)
+            nc.vector.memset(fv[:, :, 0, PAD:2 * PAD], 0.0)
+            nc.vector.memset(fv[:, :, 2, T:PAD + T], 0.0)
+            nc.vector.memset(redpad[b][:], 0.0)
+        for dd in range(2):
+            nc.vector.tensor_copy(out=mask2[:, dd, dd:dd + P], in_=ident[:])
+        nc.vector.tensor_copy(out=corner[:, 0, 0:1], in_=ident[:, P - 1:P])
+        nc.vector.tensor_copy(out=corner[:, 1, P - 1:P], in_=ident[:, 0:1])
+        shift_dn = mask2[:, 1, 0:P]
+        shift_up = mask2[:, 1, 2:P + 2]
+
+        w_sb = data.tile([P, 4, C * KW], BF16, name="w_sb")
+        w_flat = weight.rearrange("o c k -> o (c k)")
+
+        def load_e(b):
+            nc.sync.dma_start(out=e_sb[b][:, :, PAD:PAD + T],
+                              in_=embedding[b].rearrange("(p a) t -> p a t", a=4))
+
+        def load_f(b):
+            fv = f_sb[b][:].rearrange("p (a k) q -> p a k q", k=KW)
+            src = feature[b].rearrange("(p a) t -> p a t", a=4)
+            for k in range(KW):
+                c0 = PAD + 1 - k
+                nc.sync.dma_start(out=fv[:, :, k, c0:c0 + T], in_=src)
+
+        load_e(0)
+        load_e(1)
+        load_f(0)
+        for ot in range(4):
+            nc.sync.dma_start(out=w_sb[:, ot, :], in_=w_flat[ot * P:(ot + 1) * P, :])
+        load_f(1)
+
+        gbank = {0: (0, 1), 1: (3, 4)}
+        qbank = {0: 2, 1: 5}
+        sbank = {0: (0, 1, 2), 1: (3, 4, 5)}
+        s_ps = {}
+
+        def gram(b):
+            for h in range(2):
+                g = bank(gbank[b][h], [P, 2, 256], "g%d%d" % (b, h))
+                for tl in range(2):
+                    tau = 2 * h + tl
+                    for a in range(4):
+                        nc.tensor.matmul(
+                            out=g[:, tl, 0:GW],
+                            lhsT=e_sb[b][:, a, PAD + P * tau:PAD + P * tau + P],
+                            rhs=e_sb[b][:, a, PAD - 1 + P * tau:PAD - 1 + P * tau + GW],
+                            start=(a == 0), stop=(a == 3))
+                pr = work.tile([P, 2, 2, GW], F32, name="pr")
+                nc.vector.tensor_tensor(
+                    out=pr[:],
+                    in0=g[:, :, 0:GW].unsqueeze(2).to_broadcast([P, 2, 2, GW]),
+                    in1=mask2[:].unsqueeze(1).to_broadcast([P, 2, 2, GW]),
+                    op=ALU.mult)
+                nc.vector.tensor_reduce(out=redpad[b][:, 1 + 2 * h:3 + 2 * h, :], in_=pr[:],
+                                        axis=AX.X, op=ALU.add)
+
+        def sims(b):
+            red = redpad[b]
+            pq = bank(qbank[b], [P, NT, 6], "pq%d" % b)
+            nc.tensor.matmul(out=pq[:, :, 0:2], lhsT=shift_dn, rhs=red[:, 1:NT + 1, :], start=True, stop=False)
+            nc.tensor.matmul(out=pq[:, :, 0:2], lhsT=corner[:, 0, :], rhs=red[:, 0:NT, :], start=False, stop=True)
+            nc.tensor.matmul(out=pq[:, :, 2:4], lhsT=ident[:], rhs=red[:, 1:NT + 1, :], start=True, stop=True)
+            nc.tensor.matmul(out=pq[:, :, 4:6], lhsT=shift_up, rhs=red[:, 1:NT + 1, :], start=True, stop=False)
+            nc.tensor.matmul(out=pq[:, :, 4:6], lhsT=corner[:, 1, :], rhs=red[:, 2:NT + 2, :], start=False, stop=True)
+            nrm = work.tile([P, NT, 3], F32, name="nrm")
+            nc.scalar.activation(out=nrm[:], in_=pq[:, :, 1:6:2], func=ACT.Sqrt)
+            nc.vector.tensor_scalar_max(out=nrm[:], in0=nrm[:], scalar1=EPS)
+            r3 = work.tile([P, NT, 3], F32, name="r3")
+            nc.vector.reciprocal(out=r3[:], in_=nrm[:])
+            s1 = work.tile([P, NT, 3], F32, name="s1")
+            nc.vector.tensor_tensor(out=s1[:], in0=pq[:, :, 2:5], in1=r3[:], op=ALU.mult)
+            sim = work.tile([P, NT, 3], F32, name="sim")
+            nc.vector.tensor_tensor(out=sim[:], in0=s1[:], in1=r3[:, :, 1:2].to_broadcast([P, NT, 3]), op=ALU.mult)
+            va = work.tile([P, NT, 3, G0], F32, name="va")
+            nc.vector.tensor_copy(out=va[:], in_=sim[:].unsqueeze(3).to_broadcast([P, NT, 3, G0]))
+            vb = work.tile([P, NT, P], F32, name="vb")
+            nc.scalar.copy(out=vb[:, :, 0:2 * G0].rearrange("p t (g w) -> p t g w", w=G0),
+                           in_=sim[:, :, 0:2].unsqueeze(3).to_broadcast([P, NT, 2, G0]))
+            nc.scalar.copy(out=vb[:, :, P - G0:P], in_=sim[:, :, 2:3].to_broadcast([P, NT, G0]))
+            vaf = va[:].rearrange("p t g w -> p t (g w)")
+            srcs = [lambda tau: vaf[:, tau, 0:P], lambda tau: vb[:, tau, :], lambda tau: vaf[:, tau, 1:P + 1]]
+            for s in range(3):
+                sp = bank(sbank[b][s], [P, T], "s%d%d" % (b, s))
+                for tau in range(NT):
+                    nc.tensor.transpose(out=sp[:, tau * P:(tau + 1) * P], in_=srcs[s](tau), identity=ident[:])
+                s_ps[(b, s)] = sp
+
+        w_grp = data.tile([P, 3, 4 * O], BF16, name="w_grp", align_bytes=64)
+        w_cod = data.tile([P, 3, O], U32, name="w_cod", align_bytes=64)
+        w_scl = data.tile([P, 3, O], U8, name="w_scl", align_bytes=64)
+
+        def weights():
+            ww = w_sb[:].bitcast(F32).rearrange("p o (q v) -> p o q v", v=6)
+            wgw = w_grp[:].bitcast(F32).rearrange("p s (o u) -> p s o u", u=2)
+            n = 0
+            for h in range(2):
+                for s in range(3):
+                    wt = bank(6 + n % 2, [P, 2, 256], "wt%d" % n)
+                    n += 1
+                    for u in range(2):
+                        for ol in range(2):
+                            nc.tensor.transpose(out=wt[:, u, ol * P:(ol + 1) * P],
+                                                in_=ww[:, 2 * h + ol, :, 2 * s + u], identity=ident[:])
+                    nc.scalar.copy(out=wgw[:, s, 256 * h:256 * h + 256, :],
+                                   in_=wt[:].rearrange("p u o -> p o u"))
+            for s in range(3):
+                nc.vector.quantize_mx(out=w_cod[:, s, :].bitcast(FP8X4), scales=w_scl[:, s, :],
+                                      in_=w_grp[:, s, :])
+
+        x_cod = [data.tile([P, 3, T], U32, name="x_cod%d" % b, align_bytes=64) for b in range(B)]
+        x_scl = [data.tile([P, 3, T], U8, name="x_scl%d" % b, align_bytes=64) for b in range(B)]
+
+        def make_x(b, s):
+            xg = work.tile([P, T, 4], BF16, name="xg", bufs=3, align_bytes=64)
+            nc.vector.tensor_tensor(
+                out=xg[:],
+                in0=f_sb[b][:, 4 * s:4 * s + 4, PAD:PAD + T].rearrange("p j t -> p t j"),
+                in1=s_ps[(b, s)][:].unsqueeze(2).to_broadcast([P, T, 4]),
+                op=ALU.mult)
+            nc.vector.quantize_mx(out=x_cod[b][:, s, :].bitcast(FP8X4), scales=x_scl[b][:, s, :],
+                                  in_=xg[:].rearrange("p t j -> p (t j)"))
+
+        def mx(acc, b, ot, s):
+            nc.tensor.matmul_mx(
+                out=acc[:],
+                lhsT=w_cod[:, s, ot * P:(ot + 1) * P].bitcast(FP8X4),
+                lhsT_scale=w_scl[:, s, ot * P:(ot + 1) * P],
+                rhs=x_cod[b][:, s, :].bitcast(FP8X4),
+                rhs_scale=x_scl[b][:, s, :],
+                start=(s == 0), stop=(s == 2))
+
+        def finish(acc, b, ot, eng):
+            ob = outp.tile([P, T], F32, name="ob")
+            if eng == 0:
+                nc.scalar.copy(out=ob[:], in_=acc[:])
+            else:
+                nc.vector.tensor_copy(out=ob[:], in_=acc[:])
+            nc.sync.dma_start(out=out[b, ot * P:(ot + 1) * P, :], in_=ob[:])
+
+        gram(0)
+        sims(0)
+        gram(1)
+        weights()
+        for s in range(3):
+            make_x(0, s)
+        sims(1)
+        for ot in range(4):
+            acc = bank(6 + ot % 2, [P, T], "acc0%d" % ot)
+            for s in range(3):
+                mx(acc, 0, ot, s)
+            finish(acc, 0, ot, 0)
+        abank = (0, 1, 2, 6)
+        accs = [bank(abank[ot], [P, T], "acc1%d" % ot) for ot in range(4)]
+        for s in range(3):
+            make_x(1, s)
+            for ot in range(4):
+                mx(accs[ot], 1, ot, s)
+        for ot in range(4):
+            finish(accs[ot], 1, ot, ot % 2)

@@ -29,9 +29,10 @@ def tile_attentionconv1d_kernel(tc, feature, embedding, weight, out):
     with ExitStack() as ctx:
         const = ctx.enter_context(tc.tile_pool(name="const", bufs=1))
         data = ctx.enter_context(tc.tile_pool(name="data", bufs=1))
-        work = ctx.enter_context(tc.tile_pool(name="work", bufs=2))
+        work = ctx.enter_context(tc.tile_pool(name="work", bufs=1))
         outp = ctx.enter_context(tc.tile_pool(name="outp", bufs=4))
         psum = ctx.enter_context(tc.psum_pool(name="psum", bufs=1))
+        ctx.enter_context(tc.manual_schedule())
 
         def bank(i, shape, name):
             return psum.tile(shape, F32, tag="bk%d" % i, name=name)
@@ -42,21 +43,21 @@ def tile_attentionconv1d_kernel(tc, feature, embedding, weight, out):
 
         ident = const.tile([P, P], F32, name="ident")
         make_identity(nc, ident[:])
-        mask2 = const.tile([P, 2, GW], F32, name="mask2")
-        nc.vector.memset(mask2[:], 0.0)
-        corner = const.tile([P, 2, P], F32, name="corner")
-        nc.vector.memset(corner[:], 0.0)
 
         e_sb = [data.tile([P, 4, ROW], BF16, name="e%d" % b) for b in range(B)]
         f_sb = [data.tile([P, 12, ROW], BF16, name="f%d" % b) for b in range(B)]
-        redpad = [data.tile([P, NT + 2, 2], F32, name="red%d" % b) for b in range(B)]
+        redpad = data.tile([P, NT + 2, B, 2], F32, name="redpad")
+        mask2 = const.tile([P, 2, GW], F32, name="mask2")
+        corner = const.tile([P, 2, P], F32, name="corner")
         for b in range(B):
             nc.vector.memset(e_sb[b][:, :, 0:PAD], 0.0)
             nc.vector.memset(e_sb[b][:, :, PAD + T:ROW], 0.0)
             fv = f_sb[b][:].rearrange("p (a k) q -> p a k q", k=KW)
             nc.vector.memset(fv[:, :, 0, PAD:2 * PAD], 0.0)
             nc.vector.memset(fv[:, :, 2, T:PAD + T], 0.0)
-            nc.vector.memset(redpad[b][:], 0.0)
+        nc.vector.memset(mask2[:], 0.0)
+        nc.vector.memset(corner[:], 0.0)
+        nc.vector.memset(redpad[:], 0.0)
         for dd in range(2):
             nc.vector.tensor_copy(out=mask2[:, dd, dd:dd + P], in_=ident[:])
         nc.vector.tensor_copy(out=corner[:, 0, 0:1], in_=ident[:, P - 1:P])
@@ -86,13 +87,14 @@ def tile_attentionconv1d_kernel(tc, feature, embedding, weight, out):
         load_f(1)
 
         gbank = {0: (0, 1), 1: (3, 4)}
-        qbank = {0: 2, 1: 5}
         sbank = {0: (0, 1, 2), 1: (3, 4, 5)}
         s_ps = {}
+        g_ps = {}
 
-        def gram(b):
-            for h in range(2):
+        def gram(b, halves):
+            for h in halves:
                 g = bank(gbank[b][h], [P, 2, 256], "g%d%d" % (b, h))
+                g_ps[(b, h)] = g
                 for tl in range(2):
                     tau = 2 * h + tl
                     for a in range(4):
@@ -101,80 +103,105 @@ def tile_attentionconv1d_kernel(tc, feature, embedding, weight, out):
                             lhsT=e_sb[b][:, a, PAD + P * tau:PAD + P * tau + P],
                             rhs=e_sb[b][:, a, PAD - 1 + P * tau:PAD - 1 + P * tau + GW],
                             start=(a == 0), stop=(a == 3))
-                pr = work.tile([P, 2, 2, GW], F32, name="pr")
-                nc.vector.tensor_tensor(
-                    out=pr[:],
-                    in0=g[:, :, 0:GW].unsqueeze(2).to_broadcast([P, 2, 2, GW]),
-                    in1=mask2[:].unsqueeze(1).to_broadcast([P, 2, 2, GW]),
-                    op=ALU.mult)
-                nc.vector.tensor_reduce(out=redpad[b][:, 1 + 2 * h:3 + 2 * h, :], in_=pr[:],
-                                        axis=AX.X, op=ALU.add)
 
-        def sims(b):
-            red = redpad[b]
-            pq = bank(qbank[b], [P, NT, 6], "pq%d" % b)
-            nc.tensor.matmul(out=pq[:, :, 0:2], lhsT=shift_dn, rhs=red[:, 1:NT + 1, :], start=True, stop=False)
-            nc.tensor.matmul(out=pq[:, :, 0:2], lhsT=corner[:, 0, :], rhs=red[:, 0:NT, :], start=False, stop=True)
-            nc.tensor.matmul(out=pq[:, :, 2:4], lhsT=ident[:], rhs=red[:, 1:NT + 1, :], start=True, stop=True)
-            nc.tensor.matmul(out=pq[:, :, 4:6], lhsT=shift_up, rhs=red[:, 1:NT + 1, :], start=True, stop=False)
-            nc.tensor.matmul(out=pq[:, :, 4:6], lhsT=corner[:, 1, :], rhs=red[:, 2:NT + 2, :], start=False, stop=True)
-            nrm = work.tile([P, NT, 3], F32, name="nrm")
-            nc.scalar.activation(out=nrm[:], in_=pq[:, :, 1:6:2], func=ACT.Sqrt)
-            nc.vector.tensor_scalar_max(out=nrm[:], in0=nrm[:], scalar1=EPS)
-            r3 = work.tile([P, NT, 3], F32, name="r3")
-            nc.vector.reciprocal(out=r3[:], in_=nrm[:])
-            s1 = work.tile([P, NT, 3], F32, name="s1")
-            nc.vector.tensor_tensor(out=s1[:], in0=pq[:, :, 2:5], in1=r3[:], op=ALU.mult)
-            sim = work.tile([P, NT, 3], F32, name="sim")
-            nc.vector.tensor_tensor(out=sim[:], in0=s1[:], in1=r3[:, :, 1:2].to_broadcast([P, NT, 3]), op=ALU.mult)
-            va = work.tile([P, NT, 3, G0], F32, name="va")
-            nc.vector.tensor_copy(out=va[:], in_=sim[:].unsqueeze(3).to_broadcast([P, NT, 3, G0]))
-            vb = work.tile([P, NT, P], F32, name="vb")
-            nc.scalar.copy(out=vb[:, :, 0:2 * G0].rearrange("p t (g w) -> p t g w", w=G0),
-                           in_=sim[:, :, 0:2].unsqueeze(3).to_broadcast([P, NT, 2, G0]))
-            nc.scalar.copy(out=vb[:, :, P - G0:P], in_=sim[:, :, 2:3].to_broadcast([P, NT, G0]))
-            vaf = va[:].rearrange("p t g w -> p t (g w)")
-            srcs = [lambda tau: vaf[:, tau, 0:P], lambda tau: vb[:, tau, :], lambda tau: vaf[:, tau, 1:P + 1]]
-            for s in range(3):
-                sp = bank(sbank[b][s], [P, T], "s%d%d" % (b, s))
-                for tau in range(NT):
-                    nc.tensor.transpose(out=sp[:, tau * P:(tau + 1) * P], in_=srcs[s](tau), identity=ident[:])
-                s_ps[(b, s)] = sp
+        pr = [work.tile([P, NT, 2, GW], F32, name="pr%d" % b) for b in range(B)]
+
+        def pick(b, h):
+            nc.vector.tensor_tensor(
+                out=pr[b][:, 2 * h:2 * h + 2],
+                in0=g_ps[(b, h)][:, :, 0:GW].unsqueeze(2).to_broadcast([P, 2, 2, GW]),
+                in1=mask2[:].unsqueeze(1).to_broadcast([P, 2, 2, GW]),
+                op=ALU.mult)
+
+        def add_up(b, h):
+            nc.vector.tensor_reduce(out=redpad[:, 1 + 2 * h:3 + 2 * h, b, :], in_=pr[b][:, 2 * h:2 * h + 2],
+                                    axis=AX.X, op=ALU.add)
+
+        qbank = (2, 5)
+        pq = {}
+        nrm = [work.tile([P, NT, 3], F32, name="nrm%d" % b) for b in range(B)]
+        r3 = [work.tile([P, NT, 3], F32, name="r3%d" % b) for b in range(B)]
+        s1 = [work.tile([P, NT, 3], F32, name="s1%d" % b) for b in range(B)]
+        sim = [work.tile([P, NT, 3], F32, name="sim%d" % b) for b in range(B)]
+
+        def shifts(b):
+            q = bank(qbank[b], [P, NT, 6], "pq%d" % b)
+            pq[b] = q
+            mid = redpad[:, 1:NT + 1, b, :]
+            lo = redpad[:, 0:NT, b, :]
+            hi = redpad[:, 2:NT + 2, b, :]
+            nc.tensor.matmul(out=q[:, :, 0:2], lhsT=shift_dn, rhs=mid, start=True, stop=False)
+            nc.tensor.matmul(out=q[:, :, 0:2], lhsT=corner[:, 0, :], rhs=lo, start=False, stop=True)
+            nc.tensor.matmul(out=q[:, :, 2:4], lhsT=ident[:], rhs=mid, start=True, stop=True)
+            nc.tensor.matmul(out=q[:, :, 4:6], lhsT=shift_up, rhs=mid, start=True, stop=False)
+            nc.tensor.matmul(out=q[:, :, 4:6], lhsT=corner[:, 1, :], rhs=hi, start=False, stop=True)
+
+        def root(b):
+            nc.scalar.activation(out=nrm[b][:], in_=pq[b][:, :, 1:6:2], func=ACT.Sqrt)
+
+        def chain(b):
+            nc.vector.tensor_scalar_max(out=nrm[b][:], in0=nrm[b][:], scalar1=EPS)
+            nc.vector.reciprocal(out=r3[b][:], in_=nrm[b][:])
+            nc.vector.tensor_tensor(out=s1[b][:], in0=pq[b][:, :, 2:5], in1=r3[b][:], op=ALU.mult)
+            nc.vector.tensor_tensor(out=sim[b][:], in0=s1[b][:],
+                                    in1=r3[b][:, :, 1:2].to_broadcast([P, NT, 3]), op=ALU.mult)
+
+        va = [work.tile([P, NT, 3, G0], F32, name="va%d" % b) for b in range(B)]
+        vb = [work.tile([P, NT, P], F32, name="vb%d" % b) for b in range(B)]
+
+        def build_a(b):
+            nc.vector.tensor_copy(out=va[b][:], in_=sim[b][:].unsqueeze(3).to_broadcast([P, NT, 3, G0]))
+
+        def build_b(b):
+            nc.scalar.copy(out=vb[b][:, :, 0:2 * G0].rearrange("p t (g w) -> p t g w", w=G0),
+                           in_=sim[b][:, :, 0:2].unsqueeze(3).to_broadcast([P, NT, 2, G0]))
+            nc.scalar.copy(out=vb[b][:, :, P - G0:P], in_=sim[b][:, :, 2:3].to_broadcast([P, NT, G0]))
+
+        def spread(b, s):
+            vaf = va[b][:].rearrange("p t g w -> p t (g w)")
+            sp = bank(sbank[b][s], [P, T], "s%d%d" % (b, s))
+            for tau in range(NT):
+                src = (vaf[:, tau, 0:P], vb[b][:, tau, :], vaf[:, tau, 1:P + 1])[s]
+                nc.tensor.transpose(out=sp[:, tau * P:(tau + 1) * P], in_=src, identity=ident[:])
+            s_ps[(b, s)] = sp
 
         w_grp = data.tile([P, 3, 4 * O], BF16, name="w_grp", align_bytes=64)
         w_cod = data.tile([P, 3, O], U32, name="w_cod", align_bytes=64)
         w_scl = data.tile([P, 3, O], U8, name="w_scl", align_bytes=64)
+        ww = w_sb[:].bitcast(F32).rearrange("p o (q v) -> p o q v", v=6)
+        wgw = w_grp[:].bitcast(F32).rearrange("p s (o u) -> p s o u", u=2)
+        wt_ps = {}
 
-        def weights():
-            ww = w_sb[:].bitcast(F32).rearrange("p o (q v) -> p o q v", v=6)
-            wgw = w_grp[:].bitcast(F32).rearrange("p s (o u) -> p s o u", u=2)
-            n = 0
-            for h in range(2):
-                for s in range(3):
-                    wt = bank(6 + n % 2, [P, 2, 256], "wt%d" % n)
-                    n += 1
-                    for u in range(2):
-                        for ol in range(2):
-                            nc.tensor.transpose(out=wt[:, u, ol * P:(ol + 1) * P],
-                                                in_=ww[:, 2 * h + ol, :, 2 * s + u], identity=ident[:])
-                    nc.scalar.copy(out=wgw[:, s, 256 * h:256 * h + 256, :],
-                                   in_=wt[:].rearrange("p u o -> p o u"))
-            for s in range(3):
-                nc.vector.quantize_mx(out=w_cod[:, s, :].bitcast(FP8X4), scales=w_scl[:, s, :],
-                                      in_=w_grp[:, s, :])
+        def w_flip(h, s):
+            wt = bank(6 + (3 * h + s) % 2, [P, 2, 256], "wt%d%d" % (h, s))
+            wt_ps[(h, s)] = wt
+            for u in range(2):
+                for ol in range(2):
+                    nc.tensor.transpose(out=wt[:, u, ol * P:(ol + 1) * P],
+                                        in_=ww[:, 2 * h + ol, :, 2 * s + u], identity=ident[:])
+
+        def w_out(h, s):
+            nc.scalar.copy(out=wgw[:, s, 256 * h:256 * h + 256, :],
+                           in_=wt_ps[(h, s)][:].rearrange("p u o -> p o u"))
+
+        def w_quant(s):
+            nc.vector.quantize_mx(out=w_cod[:, s, :].bitcast(FP8X4), scales=w_scl[:, s, :], in_=w_grp[:, s, :])
 
         x_cod = [data.tile([P, 3, T], U32, name="x_cod%d" % b, align_bytes=64) for b in range(B)]
         x_scl = [data.tile([P, 3, T], U8, name="x_scl%d" % b, align_bytes=64) for b in range(B)]
+        xg = {}
 
-        def make_x(b, s):
-            xg = work.tile([P, T, 4], BF16, name="xg", bufs=3, align_bytes=64)
+        def x_mul(b, s):
+            xg[(b, s)] = work.tile([P, T, 4], BF16, name="xg%d%d" % (b, s), tag="xg", bufs=3, align_bytes=64)
             nc.vector.tensor_tensor(
-                out=xg[:],
+                out=xg[(b, s)][:],
                 in0=f_sb[b][:, 4 * s:4 * s + 4, PAD:PAD + T].rearrange("p j t -> p t j"),
                 in1=s_ps[(b, s)][:].unsqueeze(2).to_broadcast([P, T, 4]),
                 op=ALU.mult)
+
+        def x_quant(b, s):
             nc.vector.quantize_mx(out=x_cod[b][:, s, :].bitcast(FP8X4), scales=x_scl[b][:, s, :],
-                                  in_=xg[:].rearrange("p t j -> p (t j)"))
+                                  in_=xg[(b, s)][:].rearrange("p t j -> p (t j)"))
 
         def mx(acc, b, ot, s):
             nc.tensor.matmul_mx(
@@ -193,13 +220,47 @@ def tile_attentionconv1d_kernel(tc, feature, embedding, weight, out):
                 nc.vector.tensor_copy(out=ob[:], in_=acc[:])
             nc.sync.dma_start(out=out[b, ot * P:(ot + 1) * P, :], in_=ob[:])
 
-        gram(0)
-        sims(0)
-        gram(1)
-        weights()
+        gram(0, (0, 1))
+        pick(0, 0)
+        add_up(0, 0)
+        pick(0, 1)
+        add_up(0, 1)
+        gram(1, (0,))
+        shifts(0)
+        root(0)
+        pick(1, 0)
+        add_up(1, 0)
+        gram(1, (1,))
+        chain(0)
+        build_a(0)
+        build_b(0)
+        spread(0, 0)
+        pick(1, 1)
+        x_mul(0, 0)
+        add_up(1, 1)
+        spread(0, 1)
+        spread(0, 2)
         for s in range(3):
-            make_x(0, s)
-        sims(1)
+            w_flip(0, s)
+            w_out(0, s)
+        shifts(1)
+        root(1)
+        for s in range(3):
+            w_flip(1, s)
+            w_out(1, s)
+        x_mul(0, 1)
+        x_quant(0, 0)
+        chain(1)
+        build_a(1)
+        build_b(1)
+        for s in range(3):
+            spread(1, s)
+        x_mul(0, 2)
+        x_quant(0, 1)
+        for s in range(3):
+            w_quant(s)
+        x_quant(0, 2)
+        x_mul(1, 0)
         for ot in range(4):
             acc = bank(6 + ot % 2, [P, T], "acc0%d" % ot)
             for s in range(3):
@@ -207,9 +268,16 @@ def tile_attentionconv1d_kernel(tc, feature, embedding, weight, out):
             finish(acc, 0, ot, 0)
         abank = (0, 1, 2, 6)
         accs = [bank(abank[ot], [P, T], "acc1%d" % ot) for ot in range(4)]
-        for s in range(3):
-            make_x(1, s)
-            for ot in range(4):
-                mx(accs[ot], 1, ot, s)
+        x_mul(1, 1)
+        x_quant(1, 0)
+        for ot in range(4):
+            mx(accs[ot], 1, ot, 0)
+        x_mul(1, 2)
+        x_quant(1, 1)
+        for ot in range(4):
+            mx(accs[ot], 1, ot, 1)
+        x_quant(1, 2)
+        for ot in range(4):
+            mx(accs[ot], 1, ot, 2)
         for ot in range(4):
             finish(accs[ot], 1, ot, ot % 2)

@@ -194,9 +194,9 @@ def tile_attentionconv1d_kernel(tc, feature, embedding, weight, out):
         def x_mul(b, s):
             xg[(b, s)] = work.tile([P, T, 4], BF16, name="xg%d%d" % (b, s), tag="xg", bufs=3, align_bytes=64)
             nc.vector.tensor_tensor(
-                out=xg[(b, s)][:],
-                in0=f_sb[b][:, 4 * s:4 * s + 4, PAD:PAD + T].rearrange("p j t -> p t j"),
-                in1=s_ps[(b, s)][:].unsqueeze(2).to_broadcast([P, T, 4]),
+                out=xg[(b, s)][:].rearrange("p (c i) j -> p c j i", i=4),
+                in0=f_sb[b][:, 4 * s:4 * s + 4, PAD:PAD + T].rearrange("p j (c i) -> p c j i", i=4),
+                in1=s_ps[(b, s)][:].rearrange("p (c i) -> p c i", i=4).unsqueeze(2).to_broadcast([P, T // 4, 4, 4]),
                 op=ALU.mult)
 
         def x_quant(b, s):

@@ -21,6 +21,7 @@ PAD = 16
 ROW = PAD + T + PAD
 NT = T // P
 GW = 130
+NG = 4
 G0 = 43
 
 
@@ -150,7 +151,11 @@ def tile_attentionconv1d_kernel(tc, feature, embedding, weight, out):
         vb = [work.tile([P, NT, P], F32, name="vb%d" % b) for b in range(B)]
 
         def build_a(b):
-            nc.vector.tensor_copy(out=va[b][:], in_=sim[b][:].unsqueeze(3).to_broadcast([P, NT, 3, G0]))
+            src = sim[b][:].unsqueeze(3).to_broadcast([P, NT, 3, G0])
+            if b == 0:
+                nc.vector.tensor_copy(out=va[b][:], in_=src)
+            else:
+                nc.scalar.copy(out=va[b][:], in_=src)
 
         def build_b(b):
             nc.scalar.copy(out=vb[b][:, :, 0:2 * G0].rearrange("p t (g w) -> p t g w", w=G0),
@@ -199,6 +204,23 @@ def tile_attentionconv1d_kernel(tc, feature, embedding, weight, out):
                 in1=s_ps[(b, s)][:].rearrange("p (c i) -> p c i", i=4).unsqueeze(2).to_broadcast([P, T // 4, 4, 4]),
                 op=ALU.mult)
 
+        s_sb = [work.tile([P, T], F32, name="s_sb%d" % b) for b in range(B)]
+
+        def copy_s(b):
+            nc.scalar.copy(out=s_sb[b][:], in_=s_ps[(b, 2)][:])
+
+        def x_mul_g(b):
+            s = 2
+            xg[(b, s)] = work.tile([P, T, 4], BF16, name="xgp%d" % b, tag="xgp", bufs=1, align_bytes=64)
+            step = T // NG
+            for c in range(NG):
+                t0 = c * step
+                nc.gpsimd.tensor_tensor(
+                    out=xg[(b, s)][:, t0:t0 + step, :].rearrange("p (c i) j -> p c j i", i=4),
+                    in0=f_sb[b][:, 4 * s:4 * s + 4, PAD + t0:PAD + t0 + step].rearrange("p j (c i) -> p c j i", i=4),
+                    in1=s_sb[b][:, t0:t0 + step].rearrange("p (c i) -> p c i", i=4).unsqueeze(2).to_broadcast([P, step // 4, 4, 4]),
+                    op=ALU.mult)
+
         def x_quant(b, s):
             nc.vector.quantize_mx(out=x_cod[b][:, s, :].bitcast(FP8X4), scales=x_scl[b][:, s, :],
                                   in_=xg[(b, s)][:].rearrange("p t j -> p (t j)"))
@@ -235,31 +257,37 @@ def tile_attentionconv1d_kernel(tc, feature, embedding, weight, out):
         build_a(0)
         build_b(0)
         spread(0, 0)
+        spread(0, 2)
+        copy_s(0)
+        x_mul_g(0)
         pick(1, 1)
         x_mul(0, 0)
         add_up(1, 1)
         spread(0, 1)
-        spread(0, 2)
-        for s in range(3):
+        for s in range(2):
             w_flip(0, s)
             w_out(0, s)
         shifts(1)
         root(1)
-        for s in range(3):
-            w_flip(1, s)
-            w_out(1, s)
+        w_flip(0, 2)
+        w_out(0, 2)
         x_mul(0, 1)
-        x_quant(0, 0)
         chain(1)
         build_a(1)
         build_b(1)
         for s in range(3):
-            spread(1, s)
-        x_mul(0, 2)
+            w_flip(1, s)
+            w_out(1, s)
+        spread(1, 2)
+        copy_s(1)
+        spread(1, 0)
+        spread(1, 1)
+        x_quant(0, 0)
         x_quant(0, 1)
         for s in range(3):
             w_quant(s)
         x_quant(0, 2)
+        x_mul_g(1)
         x_mul(1, 0)
         for ot in range(4):
             acc = bank(6 + ot % 2, [P, T], "acc0%d" % ot)
@@ -269,15 +297,9 @@ def tile_attentionconv1d_kernel(tc, feature, embedding, weight, out):
         abank = (0, 1, 2, 6)
         accs = [bank(abank[ot], [P, T], "acc1%d" % ot) for ot in range(4)]
         x_mul(1, 1)
-        x_quant(1, 0)
-        for ot in range(4):
-            mx(accs[ot], 1, ot, 0)
-        x_mul(1, 2)
-        x_quant(1, 1)
-        for ot in range(4):
-            mx(accs[ot], 1, ot, 1)
-        x_quant(1, 2)
-        for ot in range(4):
-            mx(accs[ot], 1, ot, 2)
+        for s in range(3):
+            x_quant(1, s)
+            for ot in range(4):
+                mx(accs[ot], 1, ot, s)
         for ot in range(4):
             finish(accs[ot], 1, ot, ot % 2)

@@ -22,6 +22,7 @@ ROW = PAD + T + PAD
 NT = T // P
 GW = 130
 NG = 4
+NWARM = 4
 G0 = 43
 
 
@@ -42,29 +43,40 @@ def tile_attentionconv1d_kernel(tc, feature, embedding, weight, out):
         nc.vector.memset(warm[:, 0:1], 1.0)
         nc.scalar.activation(out=warm[:, 1:2], in_=warm[:, 0:1], func=ACT.Sqrt)
 
+        f_sb = [data.tile([P, 12, ROW], BF16, name="f%d" % b) for b in range(B)]
+        for b in range(B):
+            fv = f_sb[b][:].rearrange("p (a k) q -> p a k q", k=KW)
+            nc.vector.memset(fv[:, :, 0, PAD:2 * PAD], 0.0)
+            nc.vector.memset(fv[:, :, 2, T:PAD + T], 0.0)
+
+        zb = const.tile([P, 4 * T], BF16, name="zb", align_bytes=64)
+        zc = const.tile([P, T], U32, name="zc", align_bytes=64)
+        zs = const.tile([P, T], U8, name="zs", align_bytes=64)
+        nc.vector.memset(zb[:], 0.0)
+        nc.vector.quantize_mx(out=zc[:].bitcast(FP8X4), scales=zs[:], in_=zb[:])
+        wu = bank(7, [P, T], "wu")
+        for i in range(NWARM):
+            nc.tensor.matmul_mx(out=wu[:], lhsT=zc[:, 0:P].bitcast(FP8X4), lhsT_scale=zs[:, 0:P],
+                                rhs=zc[:].bitcast(FP8X4), rhs_scale=zs[:], start=True, stop=True)
+
         ident = const.tile([P, P], F32, name="ident")
         make_identity(nc, ident[:])
 
         e_sb = [data.tile([P, 4, ROW], BF16, name="e%d" % b) for b in range(B)]
-        f_sb = [data.tile([P, 12, ROW], BF16, name="f%d" % b) for b in range(B)]
         redpad = data.tile([P, NT + 2, B, 2], F32, name="redpad")
-        mask2 = const.tile([P, 2, GW], F32, name="mask2")
+        shifted = const.tile([P, GW], F32, name="shifted")
         corner = const.tile([P, 2, P], F32, name="corner")
         for b in range(B):
             nc.vector.memset(e_sb[b][:, :, 0:PAD], 0.0)
             nc.vector.memset(e_sb[b][:, :, PAD + T:ROW], 0.0)
-            fv = f_sb[b][:].rearrange("p (a k) q -> p a k q", k=KW)
-            nc.vector.memset(fv[:, :, 0, PAD:2 * PAD], 0.0)
-            nc.vector.memset(fv[:, :, 2, T:PAD + T], 0.0)
-        nc.vector.memset(mask2[:], 0.0)
+        nc.vector.memset(shifted[:], 0.0)
         nc.vector.memset(corner[:], 0.0)
         nc.vector.memset(redpad[:], 0.0)
-        for dd in range(2):
-            nc.vector.tensor_copy(out=mask2[:, dd, dd:dd + P], in_=ident[:])
+        nc.vector.tensor_copy(out=shifted[:, 1:P + 1], in_=ident[:])
         nc.vector.tensor_copy(out=corner[:, 0, 0:1], in_=ident[:, P - 1:P])
         nc.vector.tensor_copy(out=corner[:, 1, P - 1:P], in_=ident[:, 0:1])
-        shift_dn = mask2[:, 1, 0:P]
-        shift_up = mask2[:, 1, 2:P + 2]
+        shift_dn = shifted[:, 0:P]
+        shift_up = shifted[:, 2:P + 2]
 
         w_sb = data.tile([P, 4, C * KW], BF16, name="w_sb")
         w_flat = weight.rearrange("o c k -> o (c k)")
@@ -73,19 +85,20 @@ def tile_attentionconv1d_kernel(tc, feature, embedding, weight, out):
             nc.sync.dma_start(out=e_sb[b][:, :, PAD:PAD + T],
                               in_=embedding[b].rearrange("(p a) t -> p a t", a=4))
 
-        def load_f(b):
+        def load_f(b, a0, a1):
             fv = f_sb[b][:].rearrange("p (a k) q -> p a k q", k=KW)
             src = feature[b].rearrange("(p a) t -> p a t", a=4)
             for k in range(KW):
                 c0 = PAD + 1 - k
-                nc.sync.dma_start(out=fv[:, :, k, c0:c0 + T], in_=src)
+                nc.sync.dma_start(out=fv[:, a0:a1, k, c0:c0 + T], in_=src[:, a0:a1, :])
 
         load_e(0)
+        load_f(0, 0, 2)
         load_e(1)
-        load_f(0)
+        load_f(0, 2, 4)
         for ot in range(4):
             nc.sync.dma_start(out=w_sb[:, ot, :], in_=w_flat[ot * P:(ot + 1) * P, :])
-        load_f(1)
+        load_f(1, 0, 4)
 
         gbank = {0: (0, 1), 1: (3, 4)}
         sbank = {0: (0, 1, 2), 1: (3, 4, 5)}
@@ -105,18 +118,15 @@ def tile_attentionconv1d_kernel(tc, feature, embedding, weight, out):
                             rhs=e_sb[b][:, a, PAD - 1 + P * tau:PAD - 1 + P * tau + GW],
                             start=(a == 0), stop=(a == 3))
 
-        pr = [work.tile([P, NT, 2, GW], F32, name="pr%d" % b) for b in range(B)]
+        junk = work.tile([P, P], F32, name="junk")
 
         def pick(b, h):
-            nc.vector.tensor_tensor(
-                out=pr[b][:, 2 * h:2 * h + 2],
-                in0=g_ps[(b, h)][:, :, 0:GW].unsqueeze(2).to_broadcast([P, 2, 2, GW]),
-                in1=mask2[:].unsqueeze(1).to_broadcast([P, 2, 2, GW]),
-                op=ALU.mult)
-
-        def add_up(b, h):
-            nc.vector.tensor_reduce(out=redpad[:, 1 + 2 * h:3 + 2 * h, b, :], in_=pr[b][:, 2 * h:2 * h + 2],
-                                    axis=AX.X, op=ALU.add)
+            for tl in range(2):
+                for dd in range(2):
+                    nc.vector.scalar_tensor_tensor(
+                        out=junk[:], in0=g_ps[(b, h)][:, tl, dd:dd + P], scalar=1.0, in1=ident[:],
+                        op0=ALU.mult, op1=ALU.mult,
+                        accum_out=redpad[:, 1 + 2 * h + tl, b, dd:dd + 1])
 
         qbank = (2, 5)
         pq = {}
@@ -158,9 +168,16 @@ def tile_attentionconv1d_kernel(tc, feature, embedding, weight, out):
                 nc.scalar.copy(out=va[b][:], in_=src)
 
         def build_b(b):
-            nc.scalar.copy(out=vb[b][:, :, 0:2 * G0].rearrange("p t (g w) -> p t g w", w=G0),
-                           in_=sim[b][:, :, 0:2].unsqueeze(3).to_broadcast([P, NT, 2, G0]))
-            nc.scalar.copy(out=vb[b][:, :, P - G0:P], in_=sim[b][:, :, 2:3].to_broadcast([P, NT, G0]))
+            dst0 = vb[b][:, :, 0:2 * G0].rearrange("p t (g w) -> p t g w", w=G0)
+            src0 = sim[b][:, :, 0:2].unsqueeze(3).to_broadcast([P, NT, 2, G0])
+            dst1 = vb[b][:, :, P - G0:P]
+            src1 = sim[b][:, :, 2:3].to_broadcast([P, NT, G0])
+            if b == 0:
+                nc.vector.tensor_copy(out=dst0, in_=src0)
+                nc.vector.tensor_copy(out=dst1, in_=src1)
+            else:
+                nc.scalar.copy(out=dst0, in_=src0)
+                nc.scalar.copy(out=dst1, in_=src1)
 
         def spread(b, s):
             vaf = va[b][:].rearrange("p t g w -> p t (g w)")
@@ -196,8 +213,19 @@ def tile_attentionconv1d_kernel(tc, feature, embedding, weight, out):
         x_scl = [data.tile([P, 3, T], U8, name="x_scl%d" % b, align_bytes=64) for b in range(B)]
         xg = {}
 
+        u_sb = {}
+
+        def regroup(b, s):
+            u_sb[(b, s)] = work.tile([P, T, 4], BF16, name="u%d%d" % (b, s))
+            nc.scalar.copy(out=u_sb[(b, s)][:].rearrange("p (c i) j -> p c j i", i=4),
+                           in_=f_sb[b][:, 4 * s:4 * s + 4, PAD:PAD + T].rearrange("p j (c i) -> p c j i", i=4))
+
         def x_mul(b, s):
             xg[(b, s)] = work.tile([P, T, 4], BF16, name="xg%d%d" % (b, s), tag="xg", bufs=3, align_bytes=64)
+            if (b, s) in u_sb:
+                nc.vector.tensor_tensor(out=xg[(b, s)][:], in0=u_sb[(b, s)][:],
+                                        in1=s_ps[(b, s)][:].unsqueeze(2).to_broadcast([P, T, 4]), op=ALU.mult)
+                return
             nc.vector.tensor_tensor(
                 out=xg[(b, s)][:].rearrange("p (c i) j -> p c j i", i=4),
                 in0=f_sb[b][:, 4 * s:4 * s + 4, PAD:PAD + T].rearrange("p j (c i) -> p c j i", i=4),
@@ -244,25 +272,23 @@ def tile_attentionconv1d_kernel(tc, feature, embedding, weight, out):
 
         gram(0, (0, 1))
         pick(0, 0)
-        add_up(0, 0)
         pick(0, 1)
-        add_up(0, 1)
+        regroup(0, 0)
         gram(1, (0,))
         shifts(0)
         root(0)
         pick(1, 0)
-        add_up(1, 0)
         gram(1, (1,))
         chain(0)
         build_a(0)
         build_b(0)
+        regroup(0, 1)
         spread(0, 0)
         spread(0, 2)
         copy_s(0)
         x_mul_g(0)
-        pick(1, 1)
         x_mul(0, 0)
-        add_up(1, 1)
+        pick(1, 1)
         spread(0, 1)
         for s in range(2):
             w_flip(0, s)

@@ -21,8 +21,7 @@ PAD = 16
 ROW = PAD + T + PAD
 NT = T // P
 GW = 130
-NG = 4
-NWARM = 4
+NG_STEP = 128
 G0 = 43
 
 
@@ -48,16 +47,6 @@ def tile_attentionconv1d_kernel(tc, feature, embedding, weight, out):
             fv = f_sb[b][:].rearrange("p (a k) q -> p a k q", k=KW)
             nc.vector.memset(fv[:, :, 0, PAD:2 * PAD], 0.0)
             nc.vector.memset(fv[:, :, 2, T:PAD + T], 0.0)
-
-        zb = const.tile([P, 4 * T], BF16, name="zb", align_bytes=64)
-        zc = const.tile([P, T], U32, name="zc", align_bytes=64)
-        zs = const.tile([P, T], U8, name="zs", align_bytes=64)
-        nc.vector.memset(zb[:], 0.0)
-        nc.vector.quantize_mx(out=zc[:].bitcast(FP8X4), scales=zs[:], in_=zb[:])
-        wu = bank(7, [P, T], "wu")
-        for i in range(NWARM):
-            nc.tensor.matmul_mx(out=wu[:], lhsT=zc[:, 0:P].bitcast(FP8X4), lhsT_scale=zs[:, 0:P],
-                                rhs=zc[:].bitcast(FP8X4), rhs_scale=zs[:], start=True, stop=True)
 
         ident = const.tile([P, P], F32, name="ident")
         make_identity(nc, ident[:])
@@ -221,7 +210,7 @@ def tile_attentionconv1d_kernel(tc, feature, embedding, weight, out):
                            in_=f_sb[b][:, 4 * s:4 * s + 4, PAD:PAD + T].rearrange("p j (c i) -> p c j i", i=4))
 
         def x_mul(b, s):
-            xg[(b, s)] = work.tile([P, T, 4], BF16, name="xg%d%d" % (b, s), tag="xg", bufs=3, align_bytes=64)
+            xg[(b, s)] = work.tile([P, T, 4], BF16, name="xg%d%d" % (b, s), tag="xv%d" % s, align_bytes=64)
             if (b, s) in u_sb:
                 nc.vector.tensor_tensor(out=xg[(b, s)][:], in0=u_sb[(b, s)][:],
                                         in1=s_ps[(b, s)][:].unsqueeze(2).to_broadcast([P, T, 4]), op=ALU.mult)
@@ -237,17 +226,20 @@ def tile_attentionconv1d_kernel(tc, feature, embedding, weight, out):
         def copy_s(b):
             nc.scalar.copy(out=s_sb[b][:], in_=s_ps[(b, 2)][:])
 
-        def x_mul_g(b):
+        def x_mul_g(b, t_lo, t_hi, tag):
             s = 2
-            xg[(b, s)] = work.tile([P, T, 4], BF16, name="xgp%d" % b, tag="xgp", bufs=1, align_bytes=64)
-            step = T // NG
-            for c in range(NG):
-                t0 = c * step
+            xp = work.tile([P, t_hi - t_lo, 4], BF16, name="xg%d_%d" % (b, t_lo), tag=tag, align_bytes=64)
+            xg[(b, s, t_lo)] = xp
+            for t0 in range(t_lo, t_hi, NG_STEP):
                 nc.gpsimd.tensor_tensor(
-                    out=xg[(b, s)][:, t0:t0 + step, :].rearrange("p (c i) j -> p c j i", i=4),
-                    in0=f_sb[b][:, 4 * s:4 * s + 4, PAD + t0:PAD + t0 + step].rearrange("p j (c i) -> p c j i", i=4),
-                    in1=s_sb[b][:, t0:t0 + step].rearrange("p (c i) -> p c i", i=4).unsqueeze(2).to_broadcast([P, step // 4, 4, 4]),
+                    out=xp[:, t0 - t_lo:t0 - t_lo + NG_STEP, :].rearrange("p (c i) j -> p c j i", i=4),
+                    in0=f_sb[b][:, 4 * s:4 * s + 4, PAD + t0:PAD + t0 + NG_STEP].rearrange("p j (c i) -> p c j i", i=4),
+                    in1=s_sb[b][:, t0:t0 + NG_STEP].rearrange("p (c i) -> p c i", i=4).unsqueeze(2).to_broadcast([P, NG_STEP // 4, 4, 4]),
                     op=ALU.mult)
+
+        def x_quant_g(b, t_lo, t_hi):
+            nc.vector.quantize_mx(out=x_cod[b][:, 2, t_lo:t_hi].bitcast(FP8X4), scales=x_scl[b][:, 2, t_lo:t_hi],
+                                  in_=xg[(b, 2, t_lo)][:].rearrange("p t j -> p (t j)"))
 
         def x_quant(b, s):
             nc.vector.quantize_mx(out=x_cod[b][:, s, :].bitcast(FP8X4), scales=x_scl[b][:, s, :],
@@ -286,24 +278,22 @@ def tile_attentionconv1d_kernel(tc, feature, embedding, weight, out):
         spread(0, 0)
         spread(0, 2)
         copy_s(0)
-        x_mul_g(0)
+        x_mul_g(0, 0, T, "xg")
         x_mul(0, 0)
         pick(1, 1)
         spread(0, 1)
-        for s in range(2):
-            w_flip(0, s)
-            w_out(0, s)
+        for h, s in ((0, 0), (0, 1), (0, 2), (1, 0)):
+            w_flip(h, s)
+            w_out(h, s)
         shifts(1)
         root(1)
-        w_flip(0, 2)
-        w_out(0, 2)
+        for h, s in ((1, 1), (1, 2)):
+            w_flip(h, s)
+            w_out(h, s)
         x_mul(0, 1)
         chain(1)
         build_a(1)
         build_b(1)
-        for s in range(3):
-            w_flip(1, s)
-            w_out(1, s)
         spread(1, 2)
         copy_s(1)
         spread(1, 0)
@@ -312,9 +302,12 @@ def tile_attentionconv1d_kernel(tc, feature, embedding, weight, out):
         x_quant(0, 1)
         for s in range(3):
             w_quant(s)
-        x_quant(0, 2)
-        x_mul_g(1)
+        x_quant_g(0, 0, T)
+        x_mul_g(1, 0, T // 2, "xg")
+        regroup(1, 1)
         x_mul(1, 0)
+        x_quant(1, 0)
+        x_mul_g(1, T // 2, T, "xv0")
         for ot in range(4):
             acc = bank(6 + ot % 2, [P, T], "acc0%d" % ot)
             for s in range(3):
@@ -322,10 +315,15 @@ def tile_attentionconv1d_kernel(tc, feature, embedding, weight, out):
             finish(acc, 0, ot, 0)
         abank = (0, 1, 2, 6)
         accs = [bank(abank[ot], [P, T], "acc1%d" % ot) for ot in range(4)]
+        for ot in range(4):
+            mx(accs[ot], 1, ot, 0)
         x_mul(1, 1)
-        for s in range(3):
-            x_quant(1, s)
-            for ot in range(4):
-                mx(accs[ot], 1, ot, s)
+        x_quant_g(1, 0, T // 2)
+        x_quant(1, 1)
+        for ot in range(4):
+            mx(accs[ot], 1, ot, 1)
+        x_quant_g(1, T // 2, T)
+        for ot in range(4):
+            mx(accs[ot], 1, ot, 2)
         for ot in range(4):
             finish(accs[ot], 1, ot, ot % 2)

@@ -21,7 +21,8 @@ PAD = 16
 ROW = PAD + T + PAD
 NT = T // P
 GW = 130
-NG_STEP = 128
+TG = 320
+NG_STEP = 160
 G0 = 43
 
 
@@ -224,22 +225,25 @@ def tile_attentionconv1d_kernel(tc, feature, embedding, weight, out):
         s_sb = [work.tile([P, T], F32, name="s_sb%d" % b) for b in range(B)]
 
         def copy_s(b):
-            nc.scalar.copy(out=s_sb[b][:], in_=s_ps[(b, 2)][:])
+            nc.scalar.copy(out=s_sb[b][:, 0:TG], in_=s_ps[(b, 2)][:, 0:TG])
 
-        def x_mul_g(b, t_lo, t_hi, tag):
+        def x_mul_g(b):
             s = 2
-            xp = work.tile([P, t_hi - t_lo, 4], BF16, name="xg%d_%d" % (b, t_lo), tag=tag, align_bytes=64)
-            xg[(b, s, t_lo)] = xp
-            for t0 in range(t_lo, t_hi, NG_STEP):
+            xg[(b, s)] = work.tile([P, T, 4], BF16, name="xg%d2" % b, tag="xg", align_bytes=64)
+            for t0 in range(0, TG, NG_STEP):
                 nc.gpsimd.tensor_tensor(
-                    out=xp[:, t0 - t_lo:t0 - t_lo + NG_STEP, :].rearrange("p (c i) j -> p c j i", i=4),
+                    out=xg[(b, s)][:, t0:t0 + NG_STEP, :].rearrange("p (c i) j -> p c j i", i=4),
                     in0=f_sb[b][:, 4 * s:4 * s + 4, PAD + t0:PAD + t0 + NG_STEP].rearrange("p j (c i) -> p c j i", i=4),
                     in1=s_sb[b][:, t0:t0 + NG_STEP].rearrange("p (c i) -> p c i", i=4).unsqueeze(2).to_broadcast([P, NG_STEP // 4, 4, 4]),
                     op=ALU.mult)
 
-        def x_quant_g(b, t_lo, t_hi):
-            nc.vector.quantize_mx(out=x_cod[b][:, 2, t_lo:t_hi].bitcast(FP8X4), scales=x_scl[b][:, 2, t_lo:t_hi],
-                                  in_=xg[(b, 2, t_lo)][:].rearrange("p t j -> p (t j)"))
+        def x_mul_rest(b):
+            s = 2
+            nc.vector.tensor_tensor(
+                out=xg[(b, s)][:, TG:T, :].rearrange("p (c i) j -> p c j i", i=4),
+                in0=f_sb[b][:, 4 * s:4 * s + 4, PAD + TG:PAD + T].rearrange("p j (c i) -> p c j i", i=4),
+                in1=s_ps[(b, s)][:, TG:T].rearrange("p (c i) -> p c i", i=4).unsqueeze(2).to_broadcast([P, (T - TG) // 4, 4, 4]),
+                op=ALU.mult)
 
         def x_quant(b, s):
             nc.vector.quantize_mx(out=x_cod[b][:, s, :].bitcast(FP8X4), scales=x_scl[b][:, s, :],
@@ -278,7 +282,7 @@ def tile_attentionconv1d_kernel(tc, feature, embedding, weight, out):
         spread(0, 0)
         spread(0, 2)
         copy_s(0)
-        x_mul_g(0, 0, T, "xg")
+        x_mul_g(0)
         x_mul(0, 0)
         pick(1, 1)
         spread(0, 1)
@@ -291,6 +295,7 @@ def tile_attentionconv1d_kernel(tc, feature, embedding, weight, out):
             w_flip(h, s)
             w_out(h, s)
         x_mul(0, 1)
+        x_mul_rest(0)
         chain(1)
         build_a(1)
         build_b(1)
@@ -302,12 +307,10 @@ def tile_attentionconv1d_kernel(tc, feature, embedding, weight, out):
         x_quant(0, 1)
         for s in range(3):
             w_quant(s)
-        x_quant_g(0, 0, T)
-        x_mul_g(1, 0, T // 2, "xg")
+        x_quant(0, 2)
+        x_mul_g(1)
         regroup(1, 1)
         x_mul(1, 0)
-        x_quant(1, 0)
-        x_mul_g(1, T // 2, T, "xv0")
         for ot in range(4):
             acc = bank(6 + ot % 2, [P, T], "acc0%d" % ot)
             for s in range(3):
@@ -315,15 +318,11 @@ def tile_attentionconv1d_kernel(tc, feature, embedding, weight, out):
             finish(acc, 0, ot, 0)
         abank = (0, 1, 2, 6)
         accs = [bank(abank[ot], [P, T], "acc1%d" % ot) for ot in range(4)]
-        for ot in range(4):
-            mx(accs[ot], 1, ot, 0)
         x_mul(1, 1)
-        x_quant_g(1, 0, T // 2)
-        x_quant(1, 1)
-        for ot in range(4):
-            mx(accs[ot], 1, ot, 1)
-        x_quant_g(1, T // 2, T)
-        for ot in range(4):
-            mx(accs[ot], 1, ot, 2)
+        x_mul_rest(1)
+        for s in range(3):
+            x_quant(1, s)
+            for ot in range(4):
+                mx(accs[ot], 1, ot, s)
         for ot in range(4):
             finish(accs[ot], 1, ot, ot % 2)

@@ -21,8 +21,6 @@ PAD = 16
 ROW = PAD + T + PAD
 NT = T // P
 GW = 130
-TG = 320
-NG_STEP = 160
 G0 = 43
 
 
@@ -83,8 +81,8 @@ def tile_attentionconv1d_kernel(tc, feature, embedding, weight, out):
                 nc.sync.dma_start(out=fv[:, a0:a1, k, c0:c0 + T], in_=src[:, a0:a1, :])
 
         load_e(0)
-        load_f(0, 0, 2)
         load_e(1)
+        load_f(0, 0, 2)
         load_f(0, 2, 4)
         for ot in range(4):
             nc.sync.dma_start(out=w_sb[:, ot, :], in_=w_flat[ot * P:(ot + 1) * P, :])
@@ -140,12 +138,16 @@ def tile_attentionconv1d_kernel(tc, feature, embedding, weight, out):
         def root(b):
             nc.scalar.activation(out=nrm[b][:], in_=pq[b][:, :, 1:6:2], func=ACT.Sqrt)
 
-        def chain(b):
-            nc.vector.tensor_scalar_max(out=nrm[b][:], in0=nrm[b][:], scalar1=EPS)
-            nc.vector.reciprocal(out=r3[b][:], in_=nrm[b][:])
-            nc.vector.tensor_tensor(out=s1[b][:], in0=pq[b][:, :, 2:5], in1=r3[b][:], op=ALU.mult)
-            nc.vector.tensor_tensor(out=sim[b][:], in0=s1[b][:],
-                                    in1=r3[b][:, :, 1:2].to_broadcast([P, NT, 3]), op=ALU.mult)
+        def chain(b, step):
+            if step == 0:
+                nc.vector.tensor_scalar_max(out=nrm[b][:], in0=nrm[b][:], scalar1=EPS)
+            elif step == 1:
+                nc.vector.reciprocal(out=r3[b][:], in_=nrm[b][:])
+            elif step == 2:
+                nc.vector.tensor_tensor(out=s1[b][:], in0=pq[b][:, :, 2:5], in1=r3[b][:], op=ALU.mult)
+            else:
+                nc.vector.tensor_tensor(out=sim[b][:], in0=s1[b][:],
+                                        in1=r3[b][:, :, 1:2].to_broadcast([P, NT, 3]), op=ALU.mult)
 
         va = [work.tile([P, NT, 3, G0], F32, name="va%d" % b) for b in range(B)]
         vb = [work.tile([P, NT, P], F32, name="vb%d" % b) for b in range(B)]
@@ -205,10 +207,11 @@ def tile_attentionconv1d_kernel(tc, feature, embedding, weight, out):
 
         u_sb = {}
 
-        def regroup(b, s):
-            u_sb[(b, s)] = work.tile([P, T, 4], BF16, name="u%d%d" % (b, s))
-            nc.scalar.copy(out=u_sb[(b, s)][:].rearrange("p (c i) j -> p c j i", i=4),
-                           in_=f_sb[b][:, 4 * s:4 * s + 4, PAD:PAD + T].rearrange("p j (c i) -> p c j i", i=4))
+        def regroup(b, s, t_lo, t_hi):
+            if (b, s) not in u_sb:
+                u_sb[(b, s)] = work.tile([P, T, 4], BF16, name="u%d%d" % (b, s))
+            nc.scalar.copy(out=u_sb[(b, s)][:, t_lo:t_hi, :].rearrange("p (c i) j -> p c j i", i=4),
+                           in_=f_sb[b][:, 4 * s:4 * s + 4, PAD + t_lo:PAD + t_hi].rearrange("p j (c i) -> p c j i", i=4))
 
         def x_mul(b, s):
             xg[(b, s)] = work.tile([P, T, 4], BF16, name="xg%d%d" % (b, s), tag="xv%d" % s, align_bytes=64)
@@ -220,29 +223,6 @@ def tile_attentionconv1d_kernel(tc, feature, embedding, weight, out):
                 out=xg[(b, s)][:].rearrange("p (c i) j -> p c j i", i=4),
                 in0=f_sb[b][:, 4 * s:4 * s + 4, PAD:PAD + T].rearrange("p j (c i) -> p c j i", i=4),
                 in1=s_ps[(b, s)][:].rearrange("p (c i) -> p c i", i=4).unsqueeze(2).to_broadcast([P, T // 4, 4, 4]),
-                op=ALU.mult)
-
-        s_sb = [work.tile([P, T], F32, name="s_sb%d" % b) for b in range(B)]
-
-        def copy_s(b):
-            nc.scalar.copy(out=s_sb[b][:, 0:TG], in_=s_ps[(b, 2)][:, 0:TG])
-
-        def x_mul_g(b):
-            s = 2
-            xg[(b, s)] = work.tile([P, T, 4], BF16, name="xg%d2" % b, tag="xg", align_bytes=64)
-            for t0 in range(0, TG, NG_STEP):
-                nc.gpsimd.tensor_tensor(
-                    out=xg[(b, s)][:, t0:t0 + NG_STEP, :].rearrange("p (c i) j -> p c j i", i=4),
-                    in0=f_sb[b][:, 4 * s:4 * s + 4, PAD + t0:PAD + t0 + NG_STEP].rearrange("p j (c i) -> p c j i", i=4),
-                    in1=s_sb[b][:, t0:t0 + NG_STEP].rearrange("p (c i) -> p c i", i=4).unsqueeze(2).to_broadcast([P, NG_STEP // 4, 4, 4]),
-                    op=ALU.mult)
-
-        def x_mul_rest(b):
-            s = 2
-            nc.vector.tensor_tensor(
-                out=xg[(b, s)][:, TG:T, :].rearrange("p (c i) j -> p c j i", i=4),
-                in0=f_sb[b][:, 4 * s:4 * s + 4, PAD + TG:PAD + T].rearrange("p j (c i) -> p c j i", i=4),
-                in1=s_ps[(b, s)][:, TG:T].rearrange("p (c i) -> p c i", i=4).unsqueeze(2).to_broadcast([P, (T - TG) // 4, 4, 4]),
                 op=ALU.mult)
 
         def x_quant(b, s):
@@ -269,60 +249,65 @@ def tile_attentionconv1d_kernel(tc, feature, embedding, weight, out):
         gram(0, (0, 1))
         pick(0, 0)
         pick(0, 1)
-        regroup(0, 0)
-        gram(1, (0,))
+        gram(1, (0, 1))
+        pick(1, 0)
+        pick(1, 1)
         shifts(0)
         root(0)
-        pick(1, 0)
-        gram(1, (1,))
-        chain(0)
-        build_a(0)
-        build_b(0)
-        regroup(0, 1)
-        spread(0, 0)
-        spread(0, 2)
-        copy_s(0)
-        x_mul_g(0)
-        x_mul(0, 0)
-        pick(1, 1)
-        spread(0, 1)
-        for h, s in ((0, 0), (0, 1), (0, 2), (1, 0)):
-            w_flip(h, s)
-            w_out(h, s)
+        regroup(0, 0, 0, T)
         shifts(1)
         root(1)
-        for h, s in ((1, 1), (1, 2)):
-            w_flip(h, s)
-            w_out(h, s)
+        regroup(0, 1, 0, T)
+        regroup(0, 2, 0, T)
+        for step in range(4):
+            chain(0, step)
+        build_a(0)
+        build_b(0)
+        for s in range(3):
+            spread(0, s)
+        for h in range(2):
+            for s in range(3):
+                w_flip(h, s)
+                w_out(h, s)
+        x_mul(0, 0)
+        chain(1, 0)
         x_mul(0, 1)
-        x_mul_rest(0)
-        chain(1)
+        chain(1, 1)
+        x_quant(0, 0)
+        chain(1, 2)
+        x_mul(0, 2)
+        chain(1, 3)
         build_a(1)
         build_b(1)
-        spread(1, 2)
-        copy_s(1)
-        spread(1, 0)
-        spread(1, 1)
-        x_quant(0, 0)
+        for s in range(3):
+            spread(1, s)
         x_quant(0, 1)
         for s in range(3):
             w_quant(s)
         x_quant(0, 2)
-        x_mul_g(1)
-        regroup(1, 1)
-        x_mul(1, 0)
+        regroup(1, 1, 0, T)
+        regroup(1, 2, 0, T)
+        bank0 = (6, 7, 0, 1)
+        acc0 = []
         for ot in range(4):
-            acc = bank(6 + ot % 2, [P, T], "acc0%d" % ot)
+            acc0.append(bank(bank0[ot], [P, T], "acc0%d" % ot))
             for s in range(3):
-                mx(acc, 0, ot, s)
-            finish(acc, 0, ot, 0)
-        abank = (0, 1, 2, 6)
-        accs = [bank(abank[ot], [P, T], "acc1%d" % ot) for ot in range(4)]
+                mx(acc0[ot], 0, ot, s)
+        for ot in range(4):
+            finish(acc0[ot], 0, ot, 0)
+        bank1 = (2, 6, 7, 0)
+        accs = [bank(bank1[ot], [P, T], "acc1%d" % ot) for ot in range(4)]
+        x_mul(1, 0)
         x_mul(1, 1)
-        x_mul_rest(1)
-        for s in range(3):
-            x_quant(1, s)
-            for ot in range(4):
-                mx(accs[ot], 1, ot, s)
+        x_quant(1, 0)
+        for ot in range(4):
+            mx(accs[ot], 1, ot, 0)
+        x_mul(1, 2)
+        x_quant(1, 1)
+        for ot in range(4):
+            mx(accs[ot], 1, ot, 1)
+        x_quant(1, 2)
+        for ot in range(4):
+            mx(accs[ot], 1, ot, 2)
         for ot in range(4):
             finish(accs[ot], 1, ot, ot % 2)

from contextlib import ExitStack

import concourse.mybir as mybir
from concourse.masks import make_identity

F32 = mybir.dt.float32
BF16 = mybir.dt.bfloat16
U32 = mybir.dt.uint32
U8 = mybir.dt.uint8
FP8X4 = mybir.dt.float8_e4m3fn_x4
ALU = mybir.AluOpType
ACT = mybir.ActivationFunctionType
AX = mybir.AxisListType

B, C, T, O, KW = 2, 512, 512, 512, 3
P = 128
EPS = 1e-8
FLOPS = 2 * B * O * T * C * KW

PAD = 16
ROW = PAD + T + PAD
NT = T // P
GW = 130
G0 = 43


def tile_attentionconv1d_kernel(tc, feature, embedding, weight, out):
    nc = tc.nc
    with ExitStack() as ctx:
        const = ctx.enter_context(tc.tile_pool(name="const", bufs=1))
        data = ctx.enter_context(tc.tile_pool(name="data", bufs=1))
        work = ctx.enter_context(tc.tile_pool(name="work", bufs=1))
        outp = ctx.enter_context(tc.tile_pool(name="outp", bufs=4))
        psum = ctx.enter_context(tc.psum_pool(name="psum", bufs=1))
        ctx.enter_context(tc.manual_schedule())

        def bank(i, shape, name):
            return psum.tile(shape, F32, tag="bk%d" % i, name=name)

        warm = const.tile([P, 2], F32, name="warm")
        nc.vector.memset(warm[:, 0:1], 1.0)
        nc.scalar.activation(out=warm[:, 1:2], in_=warm[:, 0:1], func=ACT.Sqrt)

        f_sb = [data.tile([P, 12, ROW], BF16, name="f%d" % b) for b in range(B)]
        for b in range(B):
            fv = f_sb[b][:].rearrange("p (a k) q -> p a k q", k=KW)
            nc.vector.memset(fv[:, :, 0, PAD:2 * PAD], 0.0)
            nc.vector.memset(fv[:, :, 2, T:PAD + T], 0.0)

        ident = const.tile([P, P], F32, name="ident")
        make_identity(nc, ident[:])

        e_sb = [data.tile([P, 4, ROW], BF16, name="e%d" % b) for b in range(B)]
        redpad = data.tile([P, NT + 2, B, 2], F32, name="redpad")
        shifted = const.tile([P, GW], F32, name="shifted")
        corner = const.tile([P, 2, P], F32, name="corner")
        for b in range(B):
            nc.vector.memset(e_sb[b][:, :, 0:PAD], 0.0)
            nc.vector.memset(e_sb[b][:, :, PAD + T:ROW], 0.0)
        nc.vector.memset(shifted[:], 0.0)
        nc.vector.memset(corner[:], 0.0)
        nc.vector.memset(redpad[:], 0.0)
        nc.vector.tensor_copy(out=shifted[:, 1:P + 1], in_=ident[:])
        nc.vector.tensor_copy(out=corner[:, 0, 0:1], in_=ident[:, P - 1:P])
        nc.vector.tensor_copy(out=corner[:, 1, P - 1:P], in_=ident[:, 0:1])
        shift_dn = shifted[:, 0:P]
        shift_up = shifted[:, 2:P + 2]

        w_sb = data.tile([P, 4, C * KW], BF16, name="w_sb")
        w_flat = weight.rearrange("o c k -> o (c k)")

        def load_e(b):
            nc.sync.dma_start(out=e_sb[b][:, :, PAD:PAD + T],
                              in_=embedding[b].rearrange("(p a) t -> p a t", a=4))

        def load_f(b, a0, a1):
            fv = f_sb[b][:].rearrange("p (a k) q -> p a k q", k=KW)
            src = feature[b].rearrange("(p a) t -> p a t", a=4)
            for k in range(KW):
                c0 = PAD + 1 - k
                nc.sync.dma_start(out=fv[:, a0:a1, k, c0:c0 + T], in_=src[:, a0:a1, :])

        load_e(0)
        load_e(1)
        load_f(0, 0, 2)
        load_f(0, 2, 4)
        for ot in range(4):
            nc.sync.dma_start(out=w_sb[:, ot, :], in_=w_flat[ot * P:(ot + 1) * P, :])
        load_f(1, 0, 4)

        gbank = {0: (0, 1), 1: (3, 4)}
        sbank = {0: (0, 1, 2), 1: (3, 4, 5)}
        s_ps = {}
        g_ps = {}

        def gram(b, halves):
            for h in halves:
                g = bank(gbank[b][h], [P, 2, 256], "g%d%d" % (b, h))
                g_ps[(b, h)] = g
                for tl in range(2):
                    tau = 2 * h + tl
                    for a in range(4):
                        nc.tensor.matmul(
                            out=g[:, tl, 0:GW],
                            lhsT=e_sb[b][:, a, PAD + P * tau:PAD + P * tau + P],
                            rhs=e_sb[b][:, a, PAD - 1 + P * tau:PAD - 1 + P * tau + GW],
                            start=(a == 0), stop=(a == 3))

        junk = work.tile([P, P], F32, name="junk")

        def pick(b, h):
            for tl in range(2):
                for dd in range(2):
                    nc.vector.scalar_tensor_tensor(
                        out=junk[:], in0=g_ps[(b, h)][:, tl, dd:dd + P], scalar=1.0, in1=ident[:],
                        op0=ALU.mult, op1=ALU.mult,
                        accum_out=redpad[:, 1 + 2 * h + tl, b, dd:dd + 1])

        qbank = (2, 5)
        pq = {}
        nrm = [work.tile([P, NT, 3], F32, name="nrm%d" % b) for b in range(B)]
        r3 = [work.tile([P, NT, 3], F32, name="r3%d" % b) for b in range(B)]
        s1 = [work.tile([P, NT, 3], F32, name="s1%d" % b) for b in range(B)]
        sim = [work.tile([P, NT, 3], F32, name="sim%d" % b) for b in range(B)]

        def shifts(b):
            q = bank(qbank[b], [P, NT, 6], "pq%d" % b)
            pq[b] = q
            mid = redpad[:, 1:NT + 1, b, :]
            lo = redpad[:, 0:NT, b, :]
            hi = redpad[:, 2:NT + 2, b, :]
            nc.tensor.matmul(out=q[:, :, 0:2], lhsT=shift_dn, rhs=mid, start=True, stop=False)
            nc.tensor.matmul(out=q[:, :, 0:2], lhsT=corner[:, 0, :], rhs=lo, start=False, stop=True)
            nc.tensor.matmul(out=q[:, :, 2:4], lhsT=ident[:], rhs=mid, start=True, stop=True)
            nc.tensor.matmul(out=q[:, :, 4:6], lhsT=shift_up, rhs=mid, start=True, stop=False)
            nc.tensor.matmul(out=q[:, :, 4:6], lhsT=corner[:, 1, :], rhs=hi, start=False, stop=True)

        def root(b):
            nc.scalar.activation(out=nrm[b][:], in_=pq[b][:, :, 1:6:2], func=ACT.Sqrt)

        def chain(b, step):
            if step == 0:
                nc.vector.tensor_scalar_max(out=nrm[b][:], in0=nrm[b][:], scalar1=EPS)
            elif step == 1:
                nc.vector.reciprocal(out=r3[b][:], in_=nrm[b][:])
            elif step == 2:
                nc.vector.tensor_tensor(out=s1[b][:], in0=pq[b][:, :, 2:5], in1=r3[b][:], op=ALU.mult)
            else:
                nc.vector.tensor_tensor(out=sim[b][:], in0=s1[b][:],
                                        in1=r3[b][:, :, 1:2].to_broadcast([P, NT, 3]), op=ALU.mult)

        va = [work.tile([P, NT, 3, G0], F32, name="va%d" % b) for b in range(B)]
        vb = [work.tile([P, NT, P], F32, name="vb%d" % b) for b in range(B)]

        def build_a(b):
            src = sim[b][:].unsqueeze(3).to_broadcast([P, NT, 3, G0])
            if b == 0:
                nc.vector.tensor_copy(out=va[b][:], in_=src)
            else:
                nc.scalar.copy(out=va[b][:], in_=src)

        def build_b(b):
            dst0 = vb[b][:, :, 0:2 * G0].rearrange("p t (g w) -> p t g w", w=G0)
            src0 = sim[b][:, :, 0:2].unsqueeze(3).to_broadcast([P, NT, 2, G0])
            dst1 = vb[b][:, :, P - G0:P]
            src1 = sim[b][:, :, 2:3].to_broadcast([P, NT, G0])
            if b == 0:
                nc.vector.tensor_copy(out=dst0, in_=src0)
                nc.vector.tensor_copy(out=dst1, in_=src1)
            else:
                nc.scalar.copy(out=dst0, in_=src0)
                nc.scalar.copy(out=dst1, in_=src1)

        def spread(b, s):
            vaf = va[b][:].rearrange("p t g w -> p t (g w)")
            sp = bank(sbank[b][s], [P, T], "s%d%d" % (b, s))
            for tau in range(NT):
                src = (vaf[:, tau, 0:P], vb[b][:, tau, :], vaf[:, tau, 1:P + 1])[s]
                nc.tensor.transpose(out=sp[:, tau * P:(tau + 1) * P], in_=src, identity=ident[:])
            s_ps[(b, s)] = sp

        w_grp = data.tile([P, 3, 4 * O], BF16, name="w_grp", align_bytes=64)
        w_cod = data.tile([P, 3, O], U32, name="w_cod", align_bytes=64)
        w_scl = data.tile([P, 3, O], U8, name="w_scl", align_bytes=64)
        ww = w_sb[:].bitcast(F32).rearrange("p o (q v) -> p o q v", v=6)
        wgw = w_grp[:].bitcast(F32).rearrange("p s (o u) -> p s o u", u=2)
        wt_ps = {}

        def w_flip(h, s):
            wt = bank(6 + (3 * h + s) % 2, [P, 2, 256], "wt%d%d" % (h, s))
            wt_ps[(h, s)] = wt
            for u in range(2):
                for ol in range(2):
                    nc.tensor.transpose(out=wt[:, u, ol * P:(ol + 1) * P],
                                        in_=ww[:, 2 * h + ol, :, 2 * s + u], identity=ident[:])

        def w_out(h, s):
            nc.scalar.copy(out=wgw[:, s, 256 * h:256 * h + 256, :],
                           in_=wt_ps[(h, s)][:].rearrange("p u o -> p o u"))

        def w_quant(s):
            nc.vector.quantize_mx(out=w_cod[:, s, :].bitcast(FP8X4), scales=w_scl[:, s, :], in_=w_grp[:, s, :])

        x_cod = [data.tile([P, 3, T], U32, name="x_cod%d" % b, align_bytes=64) for b in range(B)]
        x_scl = [data.tile([P, 3, T], U8, name="x_scl%d" % b, align_bytes=64) for b in range(B)]
        xg = {}

        u_sb = {}

        def regroup(b, s, t_lo, t_hi):
            if (b, s) not in u_sb:
                u_sb[(b, s)] = work.tile([P, T, 4], BF16, name="u%d%d" % (b, s))
            nc.scalar.copy(out=u_sb[(b, s)][:, t_lo:t_hi, :].rearrange("p (c i) j -> p c j i", i=4),
                           in_=f_sb[b][:, 4 * s:4 * s + 4, PAD + t_lo:PAD + t_hi].rearrange("p j (c i) -> p c j i", i=4))

        def x_mul(b, s):
            xg[(b, s)] = work.tile([P, T, 4], BF16, name="xg%d%d" % (b, s), tag="xv%d" % s, align_bytes=64)
            if (b, s) in u_sb:
                nc.vector.tensor_tensor(out=xg[(b, s)][:], in0=u_sb[(b, s)][:],
                                        in1=s_ps[(b, s)][:].unsqueeze(2).to_broadcast([P, T, 4]), op=ALU.mult)
                return
            nc.vector.tensor_tensor(
                out=xg[(b, s)][:].rearrange("p (c i) j -> p c j i", i=4),
                in0=f_sb[b][:, 4 * s:4 * s + 4, PAD:PAD + T].rearrange("p j (c i) -> p c j i", i=4),
                in1=s_ps[(b, s)][:].rearrange("p (c i) -> p c i", i=4).unsqueeze(2).to_broadcast([P, T // 4, 4, 4]),
                op=ALU.mult)

        def x_quant(b, s):
            nc.vector.quantize_mx(out=x_cod[b][:, s, :].bitcast(FP8X4), scales=x_scl[b][:, s, :],
                                  in_=xg[(b, s)][:].rearrange("p t j -> p (t j)"))

        def mx(acc, b, ot, s):
            nc.tensor.matmul_mx(
                out=acc[:],
                lhsT=w_cod[:, s, ot * P:(ot + 1) * P].bitcast(FP8X4),
                lhsT_scale=w_scl[:, s, ot * P:(ot + 1) * P],
                rhs=x_cod[b][:, s, :].bitcast(FP8X4),
                rhs_scale=x_scl[b][:, s, :],
                start=(s == 0), stop=(s == 2))

        def finish(acc, b, ot, eng):
            ob = outp.tile([P, T], F32, name="ob")
            if eng == 0:
                nc.scalar.copy(out=ob[:], in_=acc[:])
            else:
                nc.vector.tensor_copy(out=ob[:], in_=acc[:])
            nc.sync.dma_start(out=out[b, ot * P:(ot + 1) * P, :], in_=ob[:])

        gram(0, (0, 1))
        pick(0, 0)
        pick(0, 1)
        gram(1, (0, 1))
        pick(1, 0)
        pick(1, 1)
        shifts(0)
        root(0)
        regroup(0, 0, 0, T)
        shifts(1)
        root(1)
        regroup(0, 1, 0, T)
        regroup(0, 2, 0, T)
        for step in range(4):
            chain(0, step)
        build_a(0)
        build_b(0)
        for s in range(3):
            spread(0, s)
        for h in range(2):
            for s in range(3):
                w_flip(h, s)
                w_out(h, s)
        x_mul(0, 0)
        chain(1, 0)
        x_mul(0, 1)
        chain(1, 1)
        x_quant(0, 0)
        chain(1, 2)
        x_mul(0, 2)
        chain(1, 3)
        build_a(1)
        build_b(1)
        for s in range(3):
            spread(1, s)
        x_quant(0, 1)
        for s in range(3):
            w_quant(s)
        x_quant(0, 2)
        regroup(1, 1, 0, T)
        regroup(1, 2, 0, T)
        bank0 = (6, 7, 0, 1)
        acc0 = []
        for ot in range(4):
            acc0.append(bank(bank0[ot], [P, T], "acc0%d" % ot))
            for s in range(3):
                mx(acc0[ot], 0, ot, s)
        for ot in range(4):
            finish(acc0[ot], 0, ot, 0)
        bank1 = (2, 6, 7, 0)
        accs = [bank(bank1[ot], [P, T], "acc1%d" % ot) for ot in range(4)]
        x_mul(1, 0)
        x_mul(1, 1)
        x_quant(1, 0)
        for ot in range(4):
            mx(accs[ot], 1, ot, 0)
        x_mul(1, 2)
        x_quant(1, 1)
        for ot in range(4):
            mx(accs[ot], 1, ot, 1)
        x_quant(1, 2)
        for ot in range(4):
            mx(accs[ot], 1, ot, 2)
        for ot in range(4):
            finish(accs[ot], 1, ot, ot % 2)
